import numpy as np
import ml_dtypes


def mxq(x, axis, fmt="e4m3"):
    dtype, down = {"e4m3": (ml_dtypes.float8_e4m3fn, 7), "e5m2": (ml_dtypes.float8_e5m2, 14)}[fmt]
    v = np.moveaxis(np.asarray(x, np.float32).astype(ml_dtypes.bfloat16).astype(np.float64), axis, -1)
    blocks = v.reshape(v.shape[:-1] + (-1, 32))
    amax = np.abs(blocks).max(-1, keepdims=True)
    byte = np.maximum(np.where(amax > 0, np.frexp(amax)[1] - 1 + 127, 0) - down, 1)
    scale = np.exp2(byte - 127.0)
    codes = (blocks / scale).astype(np.float32).astype(dtype).astype(np.float64)
    return np.moveaxis((codes * scale).reshape(v.shape), -1, axis)


WIDE = False


def mx_kscale(k):
    if not WIDE:
        return np.ones(k)
    levels = np.array([10, -10, 5, -5, 0])
    a = np.random.permutation(np.resize(levels, k // 512 * 4)).reshape(k // 512, 4)
    idx = np.arange(k)
    return np.exp2(a[idx // 512, idx % 128 // 32])


BF16 = ml_dtypes.bfloat16


def bf(x):
    return np.asarray(x, np.float32).astype(BF16)


def f64(x):
    return np.asarray(x).astype(np.float64)


T, K, N = 4096, 512, 1024
KK_THRESHOLD = 1e6


def setup_inputs():
    s = mx_kscale(K)
    r = s / s.max()
    return {"inputs": bf(np.random.standard_normal((T, K)) * 4.0 / np.sqrt(K) / r),
            "weight": bf(np.random.uniform(-1.0, 1.0, (N, K)) * r),
            "bias": bf(np.random.standard_normal(N) * 0.5),
            "nmk": bf(1.0 + 0.1 * np.random.standard_normal(1)),
            "kk": bf(1.0 + 0.1 * np.random.standard_normal(1))}


def reference(inputs, weight, bias, nmk, kk):
    kk_s = f64(kk)[0]
    w = f64(weight)
    w_bin = np.where(kk_s < KK_THRESHOLD, np.tanh(w * kk_s), np.sign(w))
    out = (mxq(f64(inputs), 1, "e4m3") @ mxq(w_bin, 1, "e4m3").T) + f64(bias)
    return f64(nmk)[0] * out

@@ -1,0 +1,191 @@
+from contextlib import ExitStack
+
+import concourse.mybir as mybir
+from concourse.masks import make_identity
+
+T, K, N = 4096, 512, 1024
+FLOPS = 2 * T * K * N
+
+P = 128
+BF16 = mybir.dt.bfloat16
+F32 = mybir.dt.float32
+U32 = mybir.dt.uint32
+U8 = mybir.dt.uint8
+FP8X4 = mybir.dt.float8_e4m3fn_x4
+ALU = mybir.AluOpType
+ACT = mybir.ActivationFunctionType
+
+KK_THRESHOLD = 1.0e6
+SATURATE = 3.4e38
+
+TILES = T // P
+GROUP = 4
+GROUPS = TILES // GROUP
+X_CHUNKS = (4, 4, 8, 8, 8)
+VECTOR_PREPS = 2
+SG_BANKS = (0, 3)
+
+
+def tile_binarydense_t_kernel(tc, inputs, weight, bias, nmk, kk, out):
+    nc = tc.nc
+    with ExitStack() as ctx:
+        keep = ctx.enter_context(tc.tile_pool(name="keep", bufs=1))
+        gxp = ctx.enter_context(tc.tile_pool(name="gxp", bufs=3))
+        xqp = ctx.enter_context(tc.tile_pool(name="xqp", bufs=4))
+        outp = ctx.enter_context(tc.tile_pool(name="outp", bufs=6))
+        tps = ctx.enter_context(tc.psum_pool(name="tps", bufs=2))
+        accp = ctx.enter_context(tc.psum_pool(name="accp", bufs=6))
+
+        w_view = weight.rearrange("(g p i) k -> g p (i k)", g=4, i=2)
+        w_raw = []
+        for g in range(4):
+            w_t = keep.tile([P, 2 * K], BF16, name="w_raw%d" % g)
+            nc.sync.dma_start(out=w_t[:], in_=w_view[g])
+            w_raw.append(w_t)
+
+        kk_bf = keep.tile([P, 1], BF16, name="kk_bf")
+        nc.scalar.dma_start(out=kk_bf[:], in_=kk.partition_broadcast(P))
+        nmk_bf = keep.tile([P, 1], BF16, name="nmk_bf")
+        nc.scalar.dma_start(out=nmk_bf[:], in_=nmk.partition_broadcast(P))
+
+        x_view = inputs.rearrange("(p j) k -> p (j k)", j=TILES)
+        x_words = []
+        j0 = 0
+        for c, n_tiles in enumerate(X_CHUNKS):
+            x_t = keep.tile([P, n_tiles * K], BF16, name="x_raw%d" % c)
+            nc.sync.dma_start(out=x_t[:], in_=x_view[:, j0 * K : (j0 + n_tiles) * K])
+            for jj in range(n_tiles):
+                x_words.append((x_t[:].bitcast(F32), jj * (K // 2)))
+            j0 += n_tiles
+
+        warm = keep.tile([P, 1], F32, name="warm")
+        nc.vector.memset(warm[:], 0.0)
+        nc.scalar.activation(out=warm[:], in_=warm[:], func=ACT.Tanh)
+
+        ident = keep.tile([P, P], F32, name="ident")
+        make_identity(nc, ident[:])
+        ones = keep.tile([P, P], BF16, name="ones")
+        nc.vector.memset(ones[:], 1.0)
+        bias_row = keep.tile([P, N], BF16, name="bias_row")
+        nc.vector.memset(bias_row[:], 0.0)
+        nc.scalar.dma_start(out=bias_row[0:1, :], in_=bias.rearrange("(o n) -> o n", o=1))
+
+        far = keep.tile([P, 1], F32, name="far")
+        nc.vector.tensor_scalar(
+            out=far[:], in0=kk_bf[:], scalar1=KK_THRESHOLD, scalar2=-SATURATE,
+            op0=ALU.is_lt, op1=ALU.mult,
+        )
+        nc.vector.tensor_scalar(
+            out=far[:], in0=far[:], scalar1=SATURATE, scalar2=None, op0=ALU.add,
+        )
+        w_scale = keep.tile([P, 1], F32, name="w_scale")
+        nc.vector.scalar_tensor_tensor(
+            out=w_scale[:], in0=kk_bf[:], scalar=KK_THRESHOLD, in1=far[:],
+            op0=ALU.min, op1=ALU.add,
+        )
+        nmk32 = keep.tile([P, 1], F32, name="nmk32")
+        nc.vector.tensor_copy(out=nmk32[:], in_=nmk_bf[:])
+
+        gw = keep.tile([P, 4 * N], BF16, name="gw", align_bytes=64)
+        w_codes = keep.tile([P, N], U32, name="w_codes", align_bytes=64)
+        w_scales = keep.tile([P, N], U8, name="w_scales", align_bytes=64)
+        for g in range(4):
+            wt = tps.tile([P, 512], F32, tag="tp")
+            w32 = w_raw[g][:].bitcast(F32)
+            for s in range(4):
+                nc.tensor.transpose(
+                    wt[:, P * s : P * (s + 1)], w32[:, P * s : P * (s + 1)], ident[:]
+                )
+            nc.scalar.activation(
+                out=gw[:, 1024 * g : 1024 * (g + 1)].rearrange(
+                    "q (m s e) -> q m s e", s=4, e=2
+                ),
+                in_=wt[:].bitcast(BF16).rearrange("q (s m e) -> q m s e", s=4, e=2),
+                func=ACT.Tanh,
+                scale=w_scale[:, 0:1],
+            )
+            nc.vector.quantize_mx(
+                out=w_codes[:, 256 * g : 256 * (g + 1)].bitcast(FP8X4),
+                scales=w_scales[:, 256 * g : 256 * (g + 1)],
+                in_=gw[:, 1024 * g : 1024 * (g + 1)],
+            )
+
+        bias_sb = keep.tile([P, N], F32, name="bias_sb")
+        for h in range(2):
+            bp = accp.tile([P, 512], F32, tag="acc")
+            nc.tensor.matmul(
+                out=bp[:], lhsT=ones[:], rhs=bias_row[:, 512 * h : 512 * (h + 1)],
+                start=True, stop=True,
+            )
+            nc.vector.tensor_scalar(
+                out=bias_sb[:, 512 * h : 512 * (h + 1)], in0=bp[:],
+                scalar1=nmk32[:, 0:1], scalar2=None, op0=ALU.mult,
+            )
+
+        out_view = out.rearrange("(p j) n -> p (j n)", j=TILES)
+
+        def prep(g):
+            gx = gxp.tile([P, GROUP * K], BF16, tag="gx", align_bytes=64)
+            g32 = gx[:].bitcast(F32)
+            for a in range(2):
+                xt = tps.tile([P, 512], F32, tag="tp")
+                for t in range(2):
+                    src32, col = x_words[GROUP * g + 2 * a + t]
+                    for u in range(2):
+                        nc.tensor.transpose(
+                            xt[:, (2 * t + u) * P : (2 * t + u + 1) * P],
+                            src32[:, col + P * u : col + P * (u + 1)],
+                            ident[:],
+                        )
+                dst = g32[:, 512 * a : 512 * (a + 1)].rearrange(
+                    "q (t m u) -> q t m u", t=2, u=2
+                )
+                src = xt[:].rearrange("q (t u m) -> q t m u", t=2, u=2)
+                if g < VECTOR_PREPS:
+                    nc.vector.tensor_copy(out=dst, in_=src)
+                else:
+                    nc.scalar.copy(out=dst, in_=src)
+            codes = xqp.tile([P, GROUP * P], U32, tag="xc", align_bytes=64)
+            scales = xqp.tile([P, GROUP * P], U8, tag="xs", align_bytes=64)
+            nc.vector.quantize_mx(
+                out=codes[:].bitcast(FP8X4), scales=scales[:], in_=gx[:]
+            )
+            return codes, scales
+
+        def multiply(g, codes, scales):
+            o = outp.tile([P, GROUP * N], F32, tag="o")
+            for t in range(GROUP):
+                for h in range(2):
+                    acc = accp.tile([P, 512], F32, tag="acc")
+                    nc.tensor.matmul_mx(
+                        out=acc[:],
+                        lhsT=codes[:, P * t : P * (t + 1)].bitcast(FP8X4),
+                        lhsT_scale=scales[:, P * t : P * (t + 1)],
+                        rhs=w_codes[:, 512 * h : 512 * (h + 1)].bitcast(FP8X4),
+                        rhs_scale=w_scales[:, 512 * h : 512 * (h + 1)],
+                        start=True,
+                        stop=True,
+                    )
+                    o_cols = o[:, N * t + 512 * h : N * t + 512 * (h + 1)]
+                    b_cols = bias_sb[:, 512 * h : 512 * (h + 1)]
+                    if 2 * t + h in SG_BANKS:
+                        nc.scalar.activation(
+                            out=o_cols, in_=acc[:], func=ACT.Copy, scale=nmk32[:, 0:1]
+                        )
+                        nc.gpsimd.tensor_tensor(
+                            out=o_cols, in0=o_cols, in1=b_cols, op=ALU.add
+                        )
+                    else:
+                        nc.vector.scalar_tensor_tensor(
+                            out=o_cols, in0=acc[:], scalar=nmk32[:, 0:1], in1=b_cols,
+                            op0=ALU.mult, op1=ALU.add,
+                        )
+            nc.sync.dma_start(
+                out=out_view[:, GROUP * N * g : GROUP * N * (g + 1)], in_=o[:]
+            )
+
+        ready = [prep(0), prep(1)]
+        for g in range(GROUPS):
+            multiply(g, ready[g][0], ready[g][1])
+            if g + 2 < GROUPS:
+                ready.append(prep(g + 2))

@@ -22,8 +22,8 @@ TILES = T // P
 GROUP = 4
 GROUPS = TILES // GROUP
 X_CHUNKS = (4, 4, 8, 8, 8)
-VECTOR_PREPS = 2
-SG_BANKS = (0, 3)
+S_BANKS = ((0, 2, 5), (0, 3))
+SPLIT_STORES = (0,)
 
 
 def tile_binarydense_t_kernel(tc, inputs, weight, bias, nmk, kk, out):
@@ -33,42 +33,60 @@ def tile_binarydense_t_kernel(tc, inputs, weight, bias, nmk, kk, out):
         gxp = ctx.enter_context(tc.tile_pool(name="gxp", bufs=3))
         xqp = ctx.enter_context(tc.tile_pool(name="xqp", bufs=4))
         outp = ctx.enter_context(tc.tile_pool(name="outp", bufs=6))
-        tps = ctx.enter_context(tc.psum_pool(name="tps", bufs=2))
-        accp = ctx.enter_context(tc.psum_pool(name="accp", bufs=6))
+        psum = ctx.enter_context(tc.psum_pool(name="psum", bufs=1))
+        ctx.enter_context(tc.manual_schedule())
+
+        def bank(i):
+            return psum.tile([P, 512], F32, tag="ps%d" % (i % 8), name="ps%d" % (i % 8))
 
         w_view = weight.rearrange("(g p i) k -> g p (i k)", g=4, i=2)
-        w_raw = []
-        for g in range(4):
-            w_t = keep.tile([P, 2 * K], BF16, name="w_raw%d" % g)
-            nc.sync.dma_start(out=w_t[:], in_=w_view[g])
-            w_raw.append(w_t)
+        x_view = inputs.rearrange("(p j) k -> p (j k)", j=TILES)
+        w_raw = [keep.tile([P, 2 * K], BF16, name="w_raw%d" % g) for g in range(4)]
+        x_raw = [
+            keep.tile([P, n_tiles * K], BF16, name="x_raw%d" % c)
+            for c, n_tiles in enumerate(X_CHUNKS)
+        ]
+        x_words = []
+        x_first = []
+        j0 = 0
+        for c, n_tiles in enumerate(X_CHUNKS):
+            x_first.append(j0)
+            for jj in range(n_tiles):
+                x_words.append((x_raw[c][:].bitcast(F32), jj * (K // 2)))
+            j0 += n_tiles
+
+        def load_w(g):
+            nc.sync.dma_start(out=w_raw[g][:], in_=w_view[g])
+
+        def load_x(c):
+            nc.sync.dma_start(
+                out=x_raw[c][:],
+                in_=x_view[:, x_first[c] * K : (x_first[c] + X_CHUNKS[c]) * K],
+            )
+
+        load_w(0)
+        load_w(1)
+        load_x(0)
+        load_w(2)
+        load_w(3)
+        for c in range(1, len(X_CHUNKS)):
+            load_x(c)
 
         kk_bf = keep.tile([P, 1], BF16, name="kk_bf")
         nc.scalar.dma_start(out=kk_bf[:], in_=kk.partition_broadcast(P))
         nmk_bf = keep.tile([P, 1], BF16, name="nmk_bf")
         nc.scalar.dma_start(out=nmk_bf[:], in_=nmk.partition_broadcast(P))
-
-        x_view = inputs.rearrange("(p j) k -> p (j k)", j=TILES)
-        x_words = []
-        j0 = 0
-        for c, n_tiles in enumerate(X_CHUNKS):
-            x_t = keep.tile([P, n_tiles * K], BF16, name="x_raw%d" % c)
-            nc.sync.dma_start(out=x_t[:], in_=x_view[:, j0 * K : (j0 + n_tiles) * K])
-            for jj in range(n_tiles):
-                x_words.append((x_t[:].bitcast(F32), jj * (K // 2)))
-            j0 += n_tiles
+        bias_row = keep.tile([P, N], BF16, name="bias_row")
+        nc.vector.memset(bias_row[:], 0.0)
+        nc.scalar.dma_start(out=bias_row[0:1, :], in_=bias.rearrange("(o n) -> o n", o=1))
 
         warm = keep.tile([P, 1], F32, name="warm")
         nc.vector.memset(warm[:], 0.0)
         nc.scalar.activation(out=warm[:], in_=warm[:], func=ACT.Tanh)
-
         ident = keep.tile([P, P], F32, name="ident")
         make_identity(nc, ident[:])
         ones = keep.tile([P, P], BF16, name="ones")
         nc.vector.memset(ones[:], 1.0)
-        bias_row = keep.tile([P, N], BF16, name="bias_row")
-        nc.vector.memset(bias_row[:], 0.0)
-        nc.scalar.dma_start(out=bias_row[0:1, :], in_=bias.rearrange("(o n) -> o n", o=1))
 
         far = keep.tile([P, 1], F32, name="far")
         nc.vector.tensor_scalar(
@@ -89,8 +107,11 @@ def tile_binarydense_t_kernel(tc, inputs, weight, bias, nmk, kk, out):
         gw = keep.tile([P, 4 * N], BF16, name="gw", align_bytes=64)
         w_codes = keep.tile([P, N], U32, name="w_codes", align_bytes=64)
         w_scales = keep.tile([P, N], U8, name="w_scales", align_bytes=64)
-        for g in range(4):
-            wt = tps.tile([P, 512], F32, tag="tp")
+        bias_sb = keep.tile([P, N], F32, name="bias_sb")
+        out_view = out.rearrange("(p j) n -> p (j n)", j=TILES)
+
+        def w_tanh(g, slot):
+            wt = bank(slot)
             w32 = w_raw[g][:].bitcast(F32)
             for s in range(4):
                 nc.tensor.transpose(
@@ -104,88 +125,130 @@ def tile_binarydense_t_kernel(tc, inputs, weight, bias, nmk, kk, out):
                 func=ACT.Tanh,
                 scale=w_scale[:, 0:1],
             )
+
+        def w_quantise(g):
             nc.vector.quantize_mx(
                 out=w_codes[:, 256 * g : 256 * (g + 1)].bitcast(FP8X4),
                 scales=w_scales[:, 256 * g : 256 * (g + 1)],
                 in_=gw[:, 1024 * g : 1024 * (g + 1)],
             )
 
-        bias_sb = keep.tile([P, N], F32, name="bias_sb")
-        for h in range(2):
-            bp = accp.tile([P, 512], F32, tag="acc")
+        def x_flip(g, a, gx, slot, on_vector):
+            xt = bank(slot)
+            for t in range(2):
+                src32, col = x_words[GROUP * g + 2 * a + t]
+                for u in range(2):
+                    nc.tensor.transpose(
+                        xt[:, (2 * t + u) * P : (2 * t + u + 1) * P],
+                        src32[:, col + P * u : col + P * (u + 1)],
+                        ident[:],
+                    )
+            dst = gx[:].bitcast(F32)[:, 512 * a : 512 * (a + 1)].rearrange(
+                "q (t m u) -> q t m u", t=2, u=2
+            )
+            src = xt[:].rearrange("q (t u m) -> q t m u", t=2, u=2)
+            if on_vector:
+                nc.vector.tensor_copy(out=dst, in_=src)
+            else:
+                nc.scalar.copy(out=dst, in_=src)
+
+        def new_gx():
+            return gxp.tile([P, GROUP * K], BF16, tag="gx", name="gx", align_bytes=64)
+
+        def x_quantise(gx):
+            codes = xqp.tile([P, GROUP * P], U32, tag="xc", name="xc", align_bytes=64)
+            scales = xqp.tile([P, GROUP * P], U8, tag="xs", name="xs", align_bytes=64)
+            nc.vector.quantize_mx(out=codes[:].bitcast(FP8X4), scales=scales[:], in_=gx[:])
+            return codes, scales
+
+        def bias_matmul(h, slot):
+            bp = bank(slot)
             nc.tensor.matmul(
                 out=bp[:], lhsT=ones[:], rhs=bias_row[:, 512 * h : 512 * (h + 1)],
                 start=True, stop=True,
             )
+            return bp
+
+        def bias_scale(h, bp):
             nc.vector.tensor_scalar(
                 out=bias_sb[:, 512 * h : 512 * (h + 1)], in0=bp[:],
                 scalar1=nmk32[:, 0:1], scalar2=None, op0=ALU.mult,
             )
 
-        out_view = out.rearrange("(p j) n -> p (j n)", j=TILES)
-
-        def prep(g):
-            gx = gxp.tile([P, GROUP * K], BF16, tag="gx", align_bytes=64)
-            g32 = gx[:].bitcast(F32)
-            for a in range(2):
-                xt = tps.tile([P, 512], F32, tag="tp")
-                for t in range(2):
-                    src32, col = x_words[GROUP * g + 2 * a + t]
-                    for u in range(2):
-                        nc.tensor.transpose(
-                            xt[:, (2 * t + u) * P : (2 * t + u + 1) * P],
-                            src32[:, col + P * u : col + P * (u + 1)],
-                            ident[:],
-                        )
-                dst = g32[:, 512 * a : 512 * (a + 1)].rearrange(
-                    "q (t m u) -> q t m u", t=2, u=2
+        def passes(g, o, operand, first, last, slot):
+            codes, scales = operand
+            for b in range(first, last):
+                t, h = b // 2, b % 2
+                acc = bank(slot + b - first)
+                nc.tensor.matmul_mx(
+                    out=acc[:],
+                    lhsT=codes[:, P * t : P * (t + 1)].bitcast(FP8X4),
+                    lhsT_scale=scales[:, P * t : P * (t + 1)],
+                    rhs=w_codes[:, 512 * h : 512 * (h + 1)].bitcast(FP8X4),
+                    rhs_scale=w_scales[:, 512 * h : 512 * (h + 1)],
+                    start=True,
+                    stop=True,
                 )
-                src = xt[:].rearrange("q (t u m) -> q t m u", t=2, u=2)
-                if g < VECTOR_PREPS:
-                    nc.vector.tensor_copy(out=dst, in_=src)
-                else:
-                    nc.scalar.copy(out=dst, in_=src)
-            codes = xqp.tile([P, GROUP * P], U32, tag="xc", align_bytes=64)
-            scales = xqp.tile([P, GROUP * P], U8, tag="xs", align_bytes=64)
-            nc.vector.quantize_mx(
-                out=codes[:].bitcast(FP8X4), scales=scales[:], in_=gx[:]
-            )
-            return codes, scales
-
-        def multiply(g, codes, scales):
-            o = outp.tile([P, GROUP * N], F32, tag="o")
-            for t in range(GROUP):
-                for h in range(2):
-                    acc = accp.tile([P, 512], F32, tag="acc")
-                    nc.tensor.matmul_mx(
-                        out=acc[:],
-                        lhsT=codes[:, P * t : P * (t + 1)].bitcast(FP8X4),
-                        lhsT_scale=scales[:, P * t : P * (t + 1)],
-                        rhs=w_codes[:, 512 * h : 512 * (h + 1)].bitcast(FP8X4),
-                        rhs_scale=w_scales[:, 512 * h : 512 * (h + 1)],
-                        start=True,
-                        stop=True,
+                o_cols = o[:, 512 * b : 512 * (b + 1)]
+                b_cols = bias_sb[:, 512 * h : 512 * (h + 1)]
+                if b in S_BANKS[g % 2]:
+                    nc.scalar.activation(
+                        out=o_cols, in_=acc[:], func=ACT.Copy, scale=nmk32[:, 0:1]
                     )
-                    o_cols = o[:, N * t + 512 * h : N * t + 512 * (h + 1)]
-                    b_cols = bias_sb[:, 512 * h : 512 * (h + 1)]
-                    if 2 * t + h in SG_BANKS:
-                        nc.scalar.activation(
-                            out=o_cols, in_=acc[:], func=ACT.Copy, scale=nmk32[:, 0:1]
-                        )
-                        nc.gpsimd.tensor_tensor(
-                            out=o_cols, in0=o_cols, in1=b_cols, op=ALU.add
-                        )
-                    else:
-                        nc.vector.scalar_tensor_tensor(
-                            out=o_cols, in0=acc[:], scalar=nmk32[:, 0:1], in1=b_cols,
-                            op0=ALU.mult, op1=ALU.add,
-                        )
+                    nc.gpsimd.tensor_tensor(out=o_cols, in0=o_cols, in1=b_cols, op=ALU.add)
+                else:
+                    nc.vector.scalar_tensor_tensor(
+                        out=o_cols, in0=acc[:], scalar=nmk32[:, 0:1], in1=b_cols,
+                        op0=ALU.mult, op1=ALU.add,
+                    )
+
+        def store(g, o, first, last):
             nc.sync.dma_start(
-                out=out_view[:, GROUP * N * g : GROUP * N * (g + 1)], in_=o[:]
+                out=out_view[:, GROUP * N * g + 512 * first : GROUP * N * g + 512 * last],
+                in_=o[:, 512 * first : 512 * last],
             )
 
-        ready = [prep(0), prep(1)]
+        operands = {}
+        gx0 = new_gx()
+        gx1 = new_gx()
+        w_tanh(0, 0)
+        w_quantise(0)
+        w_tanh(1, 1)
+        x_flip(0, 0, gx0, 2, True)
+        w_tanh(2, 3)
+        x_flip(0, 1, gx0, 4, True)
+        w_quantise(1)
+        w_tanh(3, 5)
+        operands[0] = x_quantise(gx0)
+        w_quantise(2)
+        bp0 = bias_matmul(0, 6)
+        bp1 = bias_matmul(1, 7)
+        bias_scale(0, bp0)
+        w_quantise(3)
+        bias_scale(1, bp1)
+        x_flip(1, 0, gx1, 8, False)
+        x_flip(1, 1, gx1, 9, False)
+        slot = 10
+
         for g in range(GROUPS):
-            multiply(g, ready[g][0], ready[g][1])
+            o = outp.tile([P, GROUP * N], F32, tag="o", name="o")
+            passes(g, o, operands[g], 0, 4, slot)
+            slot += 4
+            if g in SPLIT_STORES:
+                store(g, o, 0, 4)
+            if g == 0:
+                operands[1] = x_quantise(gx1)
+            gx = None
             if g + 2 < GROUPS:
-                ready.append(prep(g + 2))
+                gx = new_gx()
+                x_flip(g + 2, 0, gx, slot, False)
+                x_flip(g + 2, 1, gx, slot + 1, False)
+                slot += 2
+            passes(g, o, operands[g], 4, 8, slot)
+            slot += 4
+            if g in SPLIT_STORES:
+                store(g, o, 4, 8)
+            else:
+                store(g, o, 0, 8)
+            if g + 2 < GROUPS:
+                operands[g + 2] = x_quantise(gx)

@@ -23,7 +23,6 @@ GROUP = 4
 GROUPS = TILES // GROUP
 X_CHUNKS = (4, 4, 8, 8, 8)
 S_BANKS = ((0, 2, 5), (0, 3))
-SPLIT_STORES = (0,)
 
 
 def tile_binarydense_t_kernel(tc, inputs, weight, bias, nmk, kk, out):
@@ -155,11 +154,23 @@ def tile_binarydense_t_kernel(tc, inputs, weight, bias, nmk, kk, out):
         def new_gx():
             return gxp.tile([P, GROUP * K], BF16, tag="gx", name="gx", align_bytes=64)
 
-        def x_quantise(gx):
+        def new_operand():
             codes = xqp.tile([P, GROUP * P], U32, tag="xc", name="xc", align_bytes=64)
             scales = xqp.tile([P, GROUP * P], U8, tag="xs", name="xs", align_bytes=64)
-            nc.vector.quantize_mx(out=codes[:].bitcast(FP8X4), scales=scales[:], in_=gx[:])
             return codes, scales
+
+        def x_quantise_part(gx, operand, first, last):
+            codes, scales = operand
+            nc.vector.quantize_mx(
+                out=codes[:, P * first : P * last].bitcast(FP8X4),
+                scales=scales[:, P * first : P * last],
+                in_=gx[:, K * first : K * last],
+            )
+
+        def x_quantise(gx):
+            operand = new_operand()
+            x_quantise_part(gx, operand, 0, GROUP)
+            return operand
 
         def bias_matmul(h, slot):
             bp = bank(slot)
@@ -175,32 +186,40 @@ def tile_binarydense_t_kernel(tc, inputs, weight, bias, nmk, kk, out):
                 scalar1=nmk32[:, 0:1], scalar2=None, op0=ALU.mult,
             )
 
-        def passes(g, o, operand, first, last, slot):
+        def one_pass(o, operand, b, slot, via_scalar):
             codes, scales = operand
-            for b in range(first, last):
-                t, h = b // 2, b % 2
-                acc = bank(slot + b - first)
-                nc.tensor.matmul_mx(
-                    out=acc[:],
-                    lhsT=codes[:, P * t : P * (t + 1)].bitcast(FP8X4),
-                    lhsT_scale=scales[:, P * t : P * (t + 1)],
-                    rhs=w_codes[:, 512 * h : 512 * (h + 1)].bitcast(FP8X4),
-                    rhs_scale=w_scales[:, 512 * h : 512 * (h + 1)],
-                    start=True,
-                    stop=True,
+            t, h = b // 2, b % 2
+            acc = bank(slot)
+            nc.tensor.matmul_mx(
+                out=acc[:],
+                lhsT=codes[:, P * t : P * (t + 1)].bitcast(FP8X4),
+                lhsT_scale=scales[:, P * t : P * (t + 1)],
+                rhs=w_codes[:, 512 * h : 512 * (h + 1)].bitcast(FP8X4),
+                rhs_scale=w_scales[:, 512 * h : 512 * (h + 1)],
+                start=True,
+                stop=True,
+            )
+            return acc
+
+        def leave(o, acc, b, via_scalar):
+            o_cols = o[:, 512 * b : 512 * (b + 1)]
+            b_cols = bias_sb[:, 512 * (b % 2) : 512 * (b % 2 + 1)]
+            if via_scalar:
+                nc.scalar.activation(
+                    out=o_cols, in_=acc[:], func=ACT.Copy, scale=nmk32[:, 0:1]
                 )
-                o_cols = o[:, 512 * b : 512 * (b + 1)]
-                b_cols = bias_sb[:, 512 * h : 512 * (h + 1)]
-                if b in S_BANKS[g % 2]:
-                    nc.scalar.activation(
-                        out=o_cols, in_=acc[:], func=ACT.Copy, scale=nmk32[:, 0:1]
-                    )
-                    nc.gpsimd.tensor_tensor(out=o_cols, in0=o_cols, in1=b_cols, op=ALU.add)
-                else:
-                    nc.vector.scalar_tensor_tensor(
-                        out=o_cols, in0=acc[:], scalar=nmk32[:, 0:1], in1=b_cols,
-                        op0=ALU.mult, op1=ALU.add,
-                    )
+                nc.gpsimd.tensor_tensor(out=o_cols, in0=o_cols, in1=b_cols, op=ALU.add)
+            else:
+                nc.vector.scalar_tensor_tensor(
+                    out=o_cols, in0=acc[:], scalar=nmk32[:, 0:1], in1=b_cols,
+                    op0=ALU.mult, op1=ALU.add,
+                )
+
+        def passes(g, o, operand, first, last, slot):
+            for b in range(first, last):
+                via_scalar = b in S_BANKS[g % 2]
+                acc = one_pass(o, operand, b, slot + b - first, via_scalar)
+                leave(o, acc, b, via_scalar)
 
         def store(g, o, first, last):
             nc.sync.dma_start(
@@ -210,45 +229,67 @@ def tile_binarydense_t_kernel(tc, inputs, weight, bias, nmk, kk, out):
 
         operands = {}
         gx0 = new_gx()
-        gx1 = new_gx()
+        operands[0] = new_operand()
+        o = outp.tile([P, GROUP * N], F32, tag="o", name="o")
         w_tanh(0, 0)
-        w_quantise(0)
         w_tanh(1, 1)
-        x_flip(0, 0, gx0, 2, True)
-        w_tanh(2, 3)
-        x_flip(0, 1, gx0, 4, True)
-        w_quantise(1)
-        w_tanh(3, 5)
-        operands[0] = x_quantise(gx0)
-        w_quantise(2)
-        bp0 = bias_matmul(0, 6)
-        bp1 = bias_matmul(1, 7)
+        bp0 = bias_matmul(0, 2)
+        bp1 = bias_matmul(1, 3)
         bias_scale(0, bp0)
-        w_quantise(3)
         bias_scale(1, bp1)
-        x_flip(1, 0, gx1, 8, False)
-        x_flip(1, 1, gx1, 9, False)
-        slot = 10
+        w_quantise(0)
+        x_flip(0, 0, gx0, 4, True)
+        w_tanh(2, 5)
+        w_quantise(1)
+        x_quantise_part(gx0, operands[0], 0, 2)
+        x_flip(0, 1, gx0, 6, True)
+        w_tanh(3, 7)
+        x_quantise_part(gx0, operands[0], 2, 4)
+        w_quantise(2)
+        acc00 = one_pass(o, operands[0], 0, 8, False)
+        acc10 = one_pass(o, operands[0], 2, 9, False)
+        acc20 = one_pass(o, operands[0], 4, 10, False)
+        acc30 = one_pass(o, operands[0], 6, 11, True)
+        leave(o, acc00, 0, False)
+        w_quantise(3)
+        leave(o, acc10, 2, False)
+        leave(o, acc30, 6, True)
+        leave(o, acc20, 4, False)
+        acc01 = one_pass(o, operands[0], 1, 12, False)
+        acc31 = one_pass(o, operands[0], 7, 13, True)
+        acc11 = one_pass(o, operands[0], 3, 14, False)
+        acc21 = one_pass(o, operands[0], 5, 15, False)
+        leave(o, acc01, 1, False)
+        store(0, o, 0, 2)
+        leave(o, acc31, 7, True)
+        leave(o, acc11, 3, False)
+        store(0, o, 2, 4)
+        leave(o, acc21, 5, False)
+        store(0, o, 4, 6)
+        store(0, o, 6, 8)
+        gx1 = new_gx()
+        x_flip(1, 0, gx1, 16, False)
+        x_flip(1, 1, gx1, 17, False)
+        gx2 = new_gx()
+        x_flip(2, 0, gx2, 18, False)
+        x_flip(2, 1, gx2, 19, False)
+        operands[1] = x_quantise(gx1)
+        slot = 20
 
-        for g in range(GROUPS):
+        for g in range(1, GROUPS):
             o = outp.tile([P, GROUP * N], F32, tag="o", name="o")
             passes(g, o, operands[g], 0, 4, slot)
             slot += 4
-            if g in SPLIT_STORES:
-                store(g, o, 0, 4)
-            if g == 0:
-                operands[1] = x_quantise(gx1)
+            if g == 1:
+                operands[2] = x_quantise(gx2)
             gx = None
-            if g + 2 < GROUPS:
+            if 2 < g + 2 < GROUPS:
                 gx = new_gx()
                 x_flip(g + 2, 0, gx, slot, False)
                 x_flip(g + 2, 1, gx, slot + 1, False)
                 slot += 2
             passes(g, o, operands[g], 4, 8, slot)
             slot += 4
-            if g in SPLIT_STORES:
-                store(g, o, 4, 8)
-            else:
-                store(g, o, 0, 8)
-            if g + 2 < GROUPS:
+            store(g, o, 0, 8)
+            if 2 < g + 2 < GROUPS:
                 operands[g + 2] = x_quantise(gx)

from contextlib import ExitStack

import concourse.mybir as mybir
from concourse.masks import make_identity

T, K, N = 4096, 512, 1024
FLOPS = 2 * T * K * N

P = 128
BF16 = mybir.dt.bfloat16
F32 = mybir.dt.float32
U32 = mybir.dt.uint32
U8 = mybir.dt.uint8
FP8X4 = mybir.dt.float8_e4m3fn_x4
ALU = mybir.AluOpType
ACT = mybir.ActivationFunctionType

KK_THRESHOLD = 1.0e6
SATURATE = 3.4e38

TILES = T // P
GROUP = 4
GROUPS = TILES // GROUP
X_CHUNKS = (4, 4, 8, 8, 8)
S_BANKS = ((0, 2, 5), (0, 3))


def tile_binarydense_t_kernel(tc, inputs, weight, bias, nmk, kk, out):
    nc = tc.nc
    with ExitStack() as ctx:
        keep = ctx.enter_context(tc.tile_pool(name="keep", bufs=1))
        gxp = ctx.enter_context(tc.tile_pool(name="gxp", bufs=3))
        xqp = ctx.enter_context(tc.tile_pool(name="xqp", bufs=4))
        outp = ctx.enter_context(tc.tile_pool(name="outp", bufs=6))
        psum = ctx.enter_context(tc.psum_pool(name="psum", bufs=1))
        ctx.enter_context(tc.manual_schedule())

        def bank(i):
            return psum.tile([P, 512], F32, tag="ps%d" % (i % 8), name="ps%d" % (i % 8))

        w_view = weight.rearrange("(g p i) k -> g p (i k)", g=4, i=2)
        x_view = inputs.rearrange("(p j) k -> p (j k)", j=TILES)
        w_raw = [keep.tile([P, 2 * K], BF16, name="w_raw%d" % g) for g in range(4)]
        x_raw = [
            keep.tile([P, n_tiles * K], BF16, name="x_raw%d" % c)
            for c, n_tiles in enumerate(X_CHUNKS)
        ]
        x_words = []
        x_first = []
        j0 = 0
        for c, n_tiles in enumerate(X_CHUNKS):
            x_first.append(j0)
            for jj in range(n_tiles):
                x_words.append((x_raw[c][:].bitcast(F32), jj * (K // 2)))
            j0 += n_tiles

        def load_w(g):
            nc.sync.dma_start(out=w_raw[g][:], in_=w_view[g])

        def load_x(c):
            nc.sync.dma_start(
                out=x_raw[c][:],
                in_=x_view[:, x_first[c] * K : (x_first[c] + X_CHUNKS[c]) * K],
            )

        load_w(0)
        load_w(1)
        load_x(0)
        load_w(2)
        load_w(3)
        for c in range(1, len(X_CHUNKS)):
            load_x(c)

        kk_bf = keep.tile([P, 1], BF16, name="kk_bf")
        nc.scalar.dma_start(out=kk_bf[:], in_=kk.partition_broadcast(P))
        nmk_bf = keep.tile([P, 1], BF16, name="nmk_bf")
        nc.scalar.dma_start(out=nmk_bf[:], in_=nmk.partition_broadcast(P))
        bias_row = keep.tile([P, N], BF16, name="bias_row")
        nc.vector.memset(bias_row[:], 0.0)
        nc.scalar.dma_start(out=bias_row[0:1, :], in_=bias.rearrange("(o n) -> o n", o=1))

        warm = keep.tile([P, 1], F32, name="warm")
        nc.vector.memset(warm[:], 0.0)
        nc.scalar.activation(out=warm[:], in_=warm[:], func=ACT.Tanh)
        ident = keep.tile([P, P], F32, name="ident")
        make_identity(nc, ident[:])
        ones = keep.tile([P, P], BF16, name="ones")
        nc.vector.memset(ones[:], 1.0)

        far = keep.tile([P, 1], F32, name="far")
        nc.vector.tensor_scalar(
            out=far[:], in0=kk_bf[:], scalar1=KK_THRESHOLD, scalar2=-SATURATE,
            op0=ALU.is_lt, op1=ALU.mult,
        )
        nc.vector.tensor_scalar(
            out=far[:], in0=far[:], scalar1=SATURATE, scalar2=None, op0=ALU.add,
        )
        w_scale = keep.tile([P, 1], F32, name="w_scale")
        nc.vector.scalar_tensor_tensor(
            out=w_scale[:], in0=kk_bf[:], scalar=KK_THRESHOLD, in1=far[:],
            op0=ALU.min, op1=ALU.add,
        )
        nmk32 = keep.tile([P, 1], F32, name="nmk32")
        nc.vector.tensor_copy(out=nmk32[:], in_=nmk_bf[:])

        gw = keep.tile([P, 4 * N], BF16, name="gw", align_bytes=64)
        w_codes = keep.tile([P, N], U32, name="w_codes", align_bytes=64)
        w_scales = keep.tile([P, N], U8, name="w_scales", align_bytes=64)
        bias_sb = keep.tile([P, N], F32, name="bias_sb")
        out_view = out.rearrange("(p j) n -> p (j n)", j=TILES)

        def w_tanh(g, slot):
            wt = bank(slot)
            w32 = w_raw[g][:].bitcast(F32)
            for s in range(4):
                nc.tensor.transpose(
                    wt[:, P * s : P * (s + 1)], w32[:, P * s : P * (s + 1)], ident[:]
                )
            nc.scalar.activation(
                out=gw[:, 1024 * g : 1024 * (g + 1)].rearrange(
                    "q (m s e) -> q m s e", s=4, e=2
                ),
                in_=wt[:].bitcast(BF16).rearrange("q (s m e) -> q m s e", s=4, e=2),
                func=ACT.Tanh,
                scale=w_scale[:, 0:1],
            )

        def w_quantise(g):
            nc.vector.quantize_mx(
                out=w_codes[:, 256 * g : 256 * (g + 1)].bitcast(FP8X4),
                scales=w_scales[:, 256 * g : 256 * (g + 1)],
                in_=gw[:, 1024 * g : 1024 * (g + 1)],
            )

        def x_flip(g, a, gx, slot, on_vector):
            xt = bank(slot)
            for t in range(2):
                src32, col = x_words[GROUP * g + 2 * a + t]
                for u in range(2):
                    nc.tensor.transpose(
                        xt[:, (2 * t + u) * P : (2 * t + u + 1) * P],
                        src32[:, col + P * u : col + P * (u + 1)],
                        ident[:],
                    )
            dst = gx[:].bitcast(F32)[:, 512 * a : 512 * (a + 1)].rearrange(
                "q (t m u) -> q t m u", t=2, u=2
            )
            src = xt[:].rearrange("q (t u m) -> q t m u", t=2, u=2)
            if on_vector:
                nc.vector.tensor_copy(out=dst, in_=src)
            else:
                nc.scalar.copy(out=dst, in_=src)

        def new_gx():
            return gxp.tile([P, GROUP * K], BF16, tag="gx", name="gx", align_bytes=64)

        def new_operand():
            codes = xqp.tile([P, GROUP * P], U32, tag="xc", name="xc", align_bytes=64)
            scales = xqp.tile([P, GROUP * P], U8, tag="xs", name="xs", align_bytes=64)
            return codes, scales

        def x_quantise_part(gx, operand, first, last):
            codes, scales = operand
            nc.vector.quantize_mx(
                out=codes[:, P * first : P * last].bitcast(FP8X4),
                scales=scales[:, P * first : P * last],
                in_=gx[:, K * first : K * last],
            )

        def x_quantise(gx):
            operand = new_operand()
            x_quantise_part(gx, operand, 0, GROUP)
            return operand

        def bias_matmul(h, slot):
            bp = bank(slot)
            nc.tensor.matmul(
                out=bp[:], lhsT=ones[:], rhs=bias_row[:, 512 * h : 512 * (h + 1)],
                start=True, stop=True,
            )
            return bp

        def bias_scale(h, bp):
            nc.vector.tensor_scalar(
                out=bias_sb[:, 512 * h : 512 * (h + 1)], in0=bp[:],
                scalar1=nmk32[:, 0:1], scalar2=None, op0=ALU.mult,
            )

        def one_pass(o, operand, b, slot, via_scalar):
            codes, scales = operand
            t, h = b // 2, b % 2
            acc = bank(slot)
            nc.tensor.matmul_mx(
                out=acc[:],
                lhsT=codes[:, P * t : P * (t + 1)].bitcast(FP8X4),
                lhsT_scale=scales[:, P * t : P * (t + 1)],
                rhs=w_codes[:, 512 * h : 512 * (h + 1)].bitcast(FP8X4),
                rhs_scale=w_scales[:, 512 * h : 512 * (h + 1)],
                start=True,
                stop=True,
            )
            return acc

        def leave(o, acc, b, via_scalar):
            o_cols = o[:, 512 * b : 512 * (b + 1)]
            b_cols = bias_sb[:, 512 * (b % 2) : 512 * (b % 2 + 1)]
            if via_scalar:
                nc.scalar.activation(
                    out=o_cols, in_=acc[:], func=ACT.Copy, scale=nmk32[:, 0:1]
                )
                nc.gpsimd.tensor_tensor(out=o_cols, in0=o_cols, in1=b_cols, op=ALU.add)
            else:
                nc.vector.scalar_tensor_tensor(
                    out=o_cols, in0=acc[:], scalar=nmk32[:, 0:1], in1=b_cols,
                    op0=ALU.mult, op1=ALU.add,
                )

        def passes(g, o, operand, first, last, slot):
            for b in range(first, last):
                via_scalar = b in S_BANKS[g % 2]
                acc = one_pass(o, operand, b, slot + b - first, via_scalar)
                leave(o, acc, b, via_scalar)

        def store(g, o, first, last):
            nc.sync.dma_start(
                out=out_view[:, GROUP * N * g + 512 * first : GROUP * N * g + 512 * last],
                in_=o[:, 512 * first : 512 * last],
            )

        operands = {}
        gx0 = new_gx()
        operands[0] = new_operand()
        o = outp.tile([P, GROUP * N], F32, tag="o", name="o")
        w_tanh(0, 0)
        w_tanh(1, 1)
        bp0 = bias_matmul(0, 2)
        bp1 = bias_matmul(1, 3)
        bias_scale(0, bp0)
        bias_scale(1, bp1)
        w_quantise(0)
        x_flip(0, 0, gx0, 4, True)
        w_tanh(2, 5)
        w_quantise(1)
        x_quantise_part(gx0, operands[0], 0, 2)
        x_flip(0, 1, gx0, 6, True)
        w_tanh(3, 7)
        x_quantise_part(gx0, operands[0], 2, 4)
        w_quantise(2)
        acc00 = one_pass(o, operands[0], 0, 8, False)
        acc10 = one_pass(o, operands[0], 2, 9, False)
        acc20 = one_pass(o, operands[0], 4, 10, False)
        acc30 = one_pass(o, operands[0], 6, 11, True)
        leave(o, acc00, 0, False)
        w_quantise(3)
        leave(o, acc10, 2, False)
        leave(o, acc30, 6, True)
        leave(o, acc20, 4, False)
        acc01 = one_pass(o, operands[0], 1, 12, False)
        acc31 = one_pass(o, operands[0], 7, 13, True)
        acc11 = one_pass(o, operands[0], 3, 14, False)
        acc21 = one_pass(o, operands[0], 5, 15, False)
        leave(o, acc01, 1, False)
        store(0, o, 0, 2)
        leave(o, acc31, 7, True)
        leave(o, acc11, 3, False)
        store(0, o, 2, 4)
        leave(o, acc21, 5, False)
        store(0, o, 4, 6)
        store(0, o, 6, 8)
        gx1 = new_gx()
        x_flip(1, 0, gx1, 16, False)
        x_flip(1, 1, gx1, 17, False)
        gx2 = new_gx()
        x_flip(2, 0, gx2, 18, False)
        x_flip(2, 1, gx2, 19, False)
        operands[1] = x_quantise(gx1)
        slot = 20

        for g in range(1, GROUPS):
            o = outp.tile([P, GROUP * N], F32, tag="o", name="o")
            passes(g, o, operands[g], 0, 4, slot)
            slot += 4
            if g == 1:
                operands[2] = x_quantise(gx2)
            gx = None
            if 2 < g + 2 < GROUPS:
                gx = new_gx()
                x_flip(g + 2, 0, gx, slot, False)
                x_flip(g + 2, 1, gx, slot + 1, False)
                slot += 2
            passes(g, o, operands[g], 4, 8, slot)
            slot += 4
            store(g, o, 0, 8)
            if 2 < g + 2 < GROUPS:
                operands[g + 2] = x_quantise(gx)
